import numpy as np
import ml_dtypes

BF16 = ml_dtypes.bfloat16


def bf(x):
    return np.asarray(x, np.float32).astype(BF16)


def f32(x):
    return np.asarray(x, np.float32)


def f64(x):
    return np.asarray(x).astype(np.float64)


def striped(idx):
    return np.tile(idx.reshape(-1, 16).T, (8, 1))


D, S, H, M, N = 128, 4096, 512, 256, 1024


def setup_inputs():
    return {"table": bf(np.random.standard_normal((D, S))), "mlp0": bf(np.random.standard_normal((D, H)) / np.sqrt(D)), "mlp1": bf(np.random.standard_normal((H, D)) / np.sqrt(H)), "unemb": bf(np.random.standard_normal((D, M)) / np.sqrt(D)), "bias": f32(0.1 * np.random.standard_normal((M, 1))), "offs": striped(np.random.permutation(np.tile(np.arange(S), 2))[:N])}


def reference(table, mlp0, mlp1, unemb, bias, offs):
    idx = offs[:16].T.reshape(-1)
    h = f64(table)[:, idx]
    y = np.maximum(f64(mlp0).T @ h, 0.0)
    r = h + f64(mlp1).T @ y
    return f64(unemb).T @ r + f64(bias)

@@ -1,0 +1,83 @@
+import concourse.mybir as mybir
+
+BF16, F32, U16 = mybir.dt.bfloat16, mybir.dt.float32, mybir.dt.uint16
+RELU = mybir.ActivationFunctionType.Relu
+IDENTITY = mybir.ActivationFunctionType.Identity
+COPY = mybir.ActivationFunctionType.Copy
+
+P = 128
+WORDS = 4096
+HIDDEN = 512
+LOGITS = 256
+TOKENS = 1024
+PIECE = 512
+HIDDEN_BLOCKS = HIDDEN // P
+LOGIT_BLOCKS = LOGITS // P
+PIECES = TOKENS // PIECE
+PIECE_OFFSET_COLUMNS = PIECE // 16
+
+FLOPS = 2 * TOKENS * (P * HIDDEN + HIDDEN * P + P * LOGITS)
+BYTES = 2 * (P * TOKENS + P * HIDDEN + HIDDEN * P + P * LOGITS) + 4 * LOGITS + 2 * P * (TOKENS // 16) + 4 * LOGITS * TOKENS
+
+
+def tile_transformermodel_kernel(tc, table, mlp0, mlp1, unemb, bias, offs, out):
+    nc = tc.nc
+    with (
+        tc.tile_pool(name="held", bufs=1) as held,
+        tc.tile_pool(name="staged", bufs=PIECES * LOGIT_BLOCKS) as staged,
+        tc.psum_pool(name="work_banks", bufs=4) as work_banks,
+        tc.psum_pool(name="logit_banks", bufs=PIECES * LOGIT_BLOCKS) as logit_banks,
+    ):
+        offsets = held.tile([P, TOKENS // 16], U16, name="offsets")
+        nc.sync.dma_start(offsets[:], offs)
+        table_sb = held.tile([P, WORDS], BF16, name="table_sb")
+        nc.sync.dma_start(table_sb[:], table)
+        mlp0_sb = held.tile([P, HIDDEN], BF16, name="mlp0_sb")
+        nc.scalar.dma_start(mlp0_sb[:], mlp0)
+        mlp1_sb = held.tile([P, HIDDEN_BLOCKS, P], BF16, name="mlp1_sb")
+        nc.sync.dma_start(mlp1_sb[:], mlp1.rearrange("(k p) d -> p k d", p=P))
+        unemb_sb = held.tile([P, LOGITS], BF16, name="unemb_sb")
+        nc.sync.dma_start(unemb_sb[:], unemb)
+        bias_sb = held.tile([P, LOGIT_BLOCKS], F32, name="bias_sb")
+        with nc.allow_non_contiguous_dma(reason="256 single float32, one to a partition"):
+            nc.sync.dma_start(bias_sb[:], bias.rearrange("(b p) o -> p (b o)", p=P))
+
+        def picked_columns(piece):
+            return table_sb[:].indirect(offsets[:, piece * PIECE_OFFSET_COLUMNS : (piece + 1) * PIECE_OFFSET_COLUMNS])
+
+
+        y_sb = [held.tile([P, HIDDEN_BLOCKS, PIECE], BF16, name=f"y_sb{piece}") for piece in range(PIECES)]
+        for piece in range(PIECES):
+            for k in range(HIDDEN_BLOCKS):
+                y_ps = work_banks.tile([P, PIECE], F32, tag="work")
+                nc.tensor.matmul(y_ps[:], mlp0_sb[:, k * P : (k + 1) * P], picked_columns(piece))
+                if k % 2 == 0:
+                    nc.vector.tensor_scalar_max(y_sb[piece][:, k, :], y_ps[:], 0.0)
+                else:
+                    nc.scalar.activation(y_sb[piece][:, k, :], y_ps[:], RELU)
+
+        logits_ps = {}
+        for piece in range(PIECES):
+            for b in range(LOGIT_BLOCKS):
+                logits_ps[piece, b] = logit_banks.tile([P, PIECE], F32, name=f"logits_ps{piece}{b}", tag="logits")
+                nc.tensor.matmul(logits_ps[piece, b][:], unemb_sb[:, b * P : (b + 1) * P], picked_columns(piece), start=True, stop=False)
+
+        z_sb = [held.tile([P, PIECE], BF16, name=f"z_sb{piece}") for piece in range(PIECES)]
+        for piece in range(PIECES):
+            z_ps = work_banks.tile([P, PIECE], F32, tag="work")
+            for k in range(HIDDEN_BLOCKS):
+                nc.tensor.matmul(z_ps[:], mlp1_sb[:, k, :], y_sb[piece][:, k, :], start=(k == 0), stop=(k == HIDDEN_BLOCKS - 1))
+            if piece % 2 == 0:
+                nc.vector.tensor_copy(z_sb[piece][:], z_ps[:])
+            else:
+                nc.scalar.activation(z_sb[piece][:], z_ps[:], COPY)
+
+        for piece in range(PIECES):
+            for b in range(LOGIT_BLOCKS):
+                nc.tensor.matmul(logits_ps[piece, b][:], unemb_sb[:, b * P : (b + 1) * P], z_sb[piece][:], start=False, stop=True)
+                out_sb = staged.tile([P, PIECE], F32, name="out_sb")
+                if b % 2 == 0:
+                    nc.vector.tensor_scalar_add(out_sb[:], logits_ps[piece, b][:], bias_sb[:, b : b + 1])
+                else:
+                    nc.scalar.activation(out_sb[:], logits_ps[piece, b][:], IDENTITY, bias=bias_sb[:, b : b + 1])
+                nc.sync.dma_start(out[b * P : (b + 1) * P, piece * PIECE : (piece + 1) * PIECE], out_sb[:])

@@ -31,16 +31,17 @@ def tile_transformermodel_kernel(tc, table, mlp0, mlp1, unemb, bias, offs, out):
         offsets = held.tile([P, TOKENS // 16], U16, name="offsets")
         nc.sync.dma_start(offsets[:], offs)
         table_sb = held.tile([P, WORDS], BF16, name="table_sb")
-        nc.sync.dma_start(table_sb[:], table)
+        nc.scalar.dma_start(table_sb[:, WORDS // 2 :], table[:, WORDS // 2 :])
+        nc.sync.dma_start(table_sb[:, : WORDS // 2], table[:, : WORDS // 2])
         mlp0_sb = held.tile([P, HIDDEN], BF16, name="mlp0_sb")
-        nc.scalar.dma_start(mlp0_sb[:], mlp0)
+        nc.gpsimd.dma_start(mlp0_sb[:], mlp0)
         mlp1_sb = held.tile([P, HIDDEN_BLOCKS, P], BF16, name="mlp1_sb")
-        nc.sync.dma_start(mlp1_sb[:], mlp1.rearrange("(k p) d -> p k d", p=P))
+        nc.gpsimd.dma_start(mlp1_sb[:], mlp1.rearrange("(k p) d -> p k d", p=P))
         unemb_sb = held.tile([P, LOGITS], BF16, name="unemb_sb")
-        nc.sync.dma_start(unemb_sb[:], unemb)
+        nc.gpsimd.dma_start(unemb_sb[:], unemb)
         bias_sb = held.tile([P, LOGIT_BLOCKS], F32, name="bias_sb")
         with nc.allow_non_contiguous_dma(reason="256 single float32, one to a partition"):
-            nc.sync.dma_start(bias_sb[:], bias.rearrange("(b p) o -> p (b o)", p=P))
+            nc.gpsimd.dma_start(bias_sb[:], bias.rearrange("(b p) o -> p (b o)", p=P))
 
         def picked_columns(piece):
             return table_sb[:].indirect(offsets[:, piece * PIECE_OFFSET_COLUMNS : (piece + 1) * PIECE_OFFSET_COLUMNS])

@@ -15,6 +15,7 @@ HIDDEN_BLOCKS = HIDDEN // P
 LOGIT_BLOCKS = LOGITS // P
 PIECES = TOKENS // PIECE
 PIECE_OFFSET_COLUMNS = PIECE // 16
+WARM_UP_MATMULS = 8
 
 FLOPS = 2 * TOKENS * (P * HIDDEN + HIDDEN * P + P * LOGITS)
 BYTES = 2 * (P * TOKENS + P * HIDDEN + HIDDEN * P + P * LOGITS) + 4 * LOGITS + 2 * P * (TOKENS // 16) + 4 * LOGITS * TOKENS
@@ -42,6 +43,12 @@ def tile_transformermodel_kernel(tc, table, mlp0, mlp1, unemb, bias, offs, out):
         bias_sb = held.tile([P, LOGIT_BLOCKS], F32, name="bias_sb")
         with nc.allow_non_contiguous_dma(reason="256 single float32, one to a partition"):
             nc.gpsimd.dma_start(bias_sb[:], bias.rearrange("(b p) o -> p (b o)", p=P))
+
+        zeros_sb = held.tile([P, PIECE], BF16, name="zeros_sb")
+        nc.vector.memset(zeros_sb[:], 0.0)
+        unread_ps = work_banks.tile([P, PIECE], F32, tag="work")
+        for turn in range(WARM_UP_MATMULS):
+            nc.tensor.matmul(unread_ps[:], zeros_sb[:, :P], zeros_sb[:])
 
         def picked_columns(piece):
             return table_sb[:].indirect(offsets[:, piece * PIECE_OFFSET_COLUMNS : (piece + 1) * PIECE_OFFSET_COLUMNS])

@@ -15,6 +15,10 @@ HIDDEN_BLOCKS = HIDDEN // P
 LOGIT_BLOCKS = LOGITS // P
 PIECES = TOKENS // PIECE
 PIECE_OFFSET_COLUMNS = PIECE // 16
+CHUNK = 256
+CHUNKS = TOKENS // CHUNK
+CHUNKS_IN_PIECE = PIECE // CHUNK
+PSUM_BANKS = 8
 WARM_UP_MATMULS = 8
 
 FLOPS = 2 * TOKENS * (P * HIDDEN + HIDDEN * P + P * LOGITS)
@@ -26,8 +30,7 @@ def tile_transformermodel_kernel(tc, table, mlp0, mlp1, unemb, bias, offs, out):
     with (
         tc.tile_pool(name="held", bufs=1) as held,
         tc.tile_pool(name="staged", bufs=PIECES * LOGIT_BLOCKS) as staged,
-        tc.psum_pool(name="work_banks", bufs=4) as work_banks,
-        tc.psum_pool(name="logit_banks", bufs=PIECES * LOGIT_BLOCKS) as logit_banks,
+        tc.psum_pool(name="banks", bufs=PSUM_BANKS) as banks,
     ):
         offsets = held.tile([P, TOKENS // 16], U16, name="offsets")
         nc.sync.dma_start(offsets[:], offs)
@@ -46,7 +49,7 @@ def tile_transformermodel_kernel(tc, table, mlp0, mlp1, unemb, bias, offs, out):
 
         zeros_sb = held.tile([P, PIECE], BF16, name="zeros_sb")
         nc.vector.memset(zeros_sb[:], 0.0)
-        unread_ps = work_banks.tile([P, PIECE], F32, tag="work")
+        unread_ps = banks.tile([P, PIECE], F32, tag="bank")
         for turn in range(WARM_UP_MATMULS):
             nc.tensor.matmul(unread_ps[:], zeros_sb[:, :P], zeros_sb[:])
 
@@ -57,32 +60,41 @@ def tile_transformermodel_kernel(tc, table, mlp0, mlp1, unemb, bias, offs, out):
         y_sb = [held.tile([P, HIDDEN_BLOCKS, PIECE], BF16, name=f"y_sb{piece}") for piece in range(PIECES)]
         for piece in range(PIECES):
             for k in range(HIDDEN_BLOCKS):
-                y_ps = work_banks.tile([P, PIECE], F32, tag="work")
+                y_ps = banks.tile([P, PIECE], F32, tag="bank")
                 nc.tensor.matmul(y_ps[:], mlp0_sb[:, k * P : (k + 1) * P], picked_columns(piece))
                 if k % 2 == 0:
                     nc.vector.tensor_scalar_max(y_sb[piece][:, k, :], y_ps[:], 0.0)
                 else:
                     nc.scalar.activation(y_sb[piece][:, k, :], y_ps[:], RELU)
 
+        z_sb = [held.tile([P, CHUNK], BF16, name=f"z_sb{chunk}") for chunk in range(CHUNKS)]
+        for chunk in range(CHUNKS):
+            piece, first = divmod(chunk * CHUNK, PIECE)
+            z_ps = banks.tile([P, PIECE], F32, tag="bank")
+            for k in range(HIDDEN_BLOCKS):
+                nc.tensor.matmul(z_ps[:, :CHUNK], mlp1_sb[:, k, :], y_sb[piece][:, k, first : first + CHUNK], start=(k == 0), stop=(k == HIDDEN_BLOCKS - 1))
+            if chunk % 2 == 0:
+                nc.vector.tensor_copy(z_sb[chunk][:], z_ps[:, :CHUNK])
+            else:
+                nc.scalar.activation(z_sb[chunk][:], z_ps[:, :CHUNK], COPY)
+
         logits_ps = {}
         for piece in range(PIECES):
             for b in range(LOGIT_BLOCKS):
-                logits_ps[piece, b] = logit_banks.tile([P, PIECE], F32, name=f"logits_ps{piece}{b}", tag="logits")
-                nc.tensor.matmul(logits_ps[piece, b][:], unemb_sb[:, b * P : (b + 1) * P], picked_columns(piece), start=True, stop=False)
-
-        z_sb = [held.tile([P, PIECE], BF16, name=f"z_sb{piece}") for piece in range(PIECES)]
-        for piece in range(PIECES):
-            z_ps = work_banks.tile([P, PIECE], F32, tag="work")
-            for k in range(HIDDEN_BLOCKS):
-                nc.tensor.matmul(z_ps[:], mlp1_sb[:, k, :], y_sb[piece][:, k, :], start=(k == 0), stop=(k == HIDDEN_BLOCKS - 1))
-            if piece % 2 == 0:
-                nc.vector.tensor_copy(z_sb[piece][:], z_ps[:])
-            else:
-                nc.scalar.activation(z_sb[piece][:], z_ps[:], COPY)
+                logits_ps[piece, b] = banks.tile([P, PIECE], F32, name=f"logits_ps{piece}{b}", tag="bank")
+            for part in range(CHUNKS_IN_PIECE):
+                for b in range(LOGIT_BLOCKS):
+                    nc.tensor.matmul(
+                        logits_ps[piece, b][:, part * CHUNK : (part + 1) * CHUNK],
+                        unemb_sb[:, b * P : (b + 1) * P],
+                        z_sb[piece * CHUNKS_IN_PIECE + part][:],
+                        start=(part == 0),
+                        stop=False,
+                    )
 
         for piece in range(PIECES):
             for b in range(LOGIT_BLOCKS):
-                nc.tensor.matmul(logits_ps[piece, b][:], unemb_sb[:, b * P : (b + 1) * P], z_sb[piece][:], start=False, stop=True)
+                nc.tensor.matmul(logits_ps[piece, b][:], unemb_sb[:, b * P : (b + 1) * P], picked_columns(piece), start=False, stop=True)
                 out_sb = staged.tile([P, PIECE], F32, name="out_sb")
                 if b % 2 == 0:
                     nc.vector.tensor_scalar_add(out_sb[:], logits_ps[piece, b][:], bias_sb[:, b : b + 1])

@@ -19,7 +19,6 @@ CHUNK = 256
 CHUNKS = TOKENS // CHUNK
 CHUNKS_IN_PIECE = PIECE // CHUNK
 PSUM_BANKS = 8
-WARM_UP_MATMULS = 8
 
 FLOPS = 2 * TOKENS * (P * HIDDEN + HIDDEN * P + P * LOGITS)
 BYTES = 2 * (P * TOKENS + P * HIDDEN + HIDDEN * P + P * LOGITS) + 4 * LOGITS + 2 * P * (TOKENS // 16) + 4 * LOGITS * TOKENS
@@ -46,12 +45,6 @@ def tile_transformermodel_kernel(tc, table, mlp0, mlp1, unemb, bias, offs, out):
         bias_sb = held.tile([P, LOGIT_BLOCKS], F32, name="bias_sb")
         with nc.allow_non_contiguous_dma(reason="256 single float32, one to a partition"):
             nc.gpsimd.dma_start(bias_sb[:], bias.rearrange("(b p) o -> p (b o)", p=P))
-
-        zeros_sb = held.tile([P, PIECE], BF16, name="zeros_sb")
-        nc.vector.memset(zeros_sb[:], 0.0)
-        unread_ps = banks.tile([P, PIECE], F32, tag="bank")
-        for turn in range(WARM_UP_MATMULS):
-            nc.tensor.matmul(unread_ps[:], zeros_sb[:, :P], zeros_sb[:])
 
         def picked_columns(piece):
             return table_sb[:].indirect(offsets[:, piece * PIECE_OFFSET_COLUMNS : (piece + 1) * PIECE_OFFSET_COLUMNS])

@@ -33,11 +33,11 @@ def tile_transformermodel_kernel(tc, table, mlp0, mlp1, unemb, bias, offs, out):
     ):
         offsets = held.tile([P, TOKENS // 16], U16, name="offsets")
         nc.sync.dma_start(offsets[:], offs)
+        mlp0_sb = held.tile([P, HIDDEN], BF16, name="mlp0_sb")
+        nc.sync.dma_start(mlp0_sb[:], mlp0)
         table_sb = held.tile([P, WORDS], BF16, name="table_sb")
         nc.scalar.dma_start(table_sb[:, WORDS // 2 :], table[:, WORDS // 2 :])
         nc.sync.dma_start(table_sb[:, : WORDS // 2], table[:, : WORDS // 2])
-        mlp0_sb = held.tile([P, HIDDEN], BF16, name="mlp0_sb")
-        nc.gpsimd.dma_start(mlp0_sb[:], mlp0)
         mlp1_sb = held.tile([P, HIDDEN_BLOCKS, P], BF16, name="mlp1_sb")
         nc.gpsimd.dma_start(mlp1_sb[:], mlp1.rearrange("(k p) d -> p k d", p=P))
         unemb_sb = held.tile([P, LOGITS], BF16, name="unemb_sb")

@@ -38,13 +38,17 @@ def tile_transformermodel_kernel(tc, table, mlp0, mlp1, unemb, bias, offs, out):
         table_sb = held.tile([P, WORDS], BF16, name="table_sb")
         nc.scalar.dma_start(table_sb[:, WORDS // 2 :], table[:, WORDS // 2 :])
         nc.sync.dma_start(table_sb[:, : WORDS // 2], table[:, : WORDS // 2])
+        table_has_landed = table_sb[:, :: WORDS // 2]
         mlp1_sb = held.tile([P, HIDDEN_BLOCKS, P], BF16, name="mlp1_sb")
-        nc.gpsimd.dma_start(mlp1_sb[:], mlp1.rearrange("(k p) d -> p k d", p=P))
+        nc.vector.tensor_copy(mlp1_sb[:, 0, :2], table_has_landed)
+        nc.sync.dma_start(mlp1_sb[:], mlp1.rearrange("(k p) d -> p k d", p=P))
         unemb_sb = held.tile([P, LOGITS], BF16, name="unemb_sb")
-        nc.gpsimd.dma_start(unemb_sb[:], unemb)
+        nc.vector.tensor_copy(unemb_sb[:, :2], table_has_landed)
+        nc.sync.dma_start(unemb_sb[:], unemb)
         bias_sb = held.tile([P, LOGIT_BLOCKS], F32, name="bias_sb")
+        nc.vector.tensor_copy(bias_sb[:], table_has_landed)
         with nc.allow_non_contiguous_dma(reason="256 single float32, one to a partition"):
-            nc.gpsimd.dma_start(bias_sb[:], bias.rearrange("(b p) o -> p (b o)", p=P))
+            nc.sync.dma_start(bias_sb[:], bias.rearrange("(b p) o -> p (b o)", p=P))
 
         def picked_columns(piece):
             return table_sb[:].indirect(offsets[:, piece * PIECE_OFFSET_COLUMNS : (piece + 1) * PIECE_OFFSET_COLUMNS])

@@ -64,37 +64,49 @@ def tile_transformermodel_kernel(tc, table, mlp0, mlp1, unemb, bias, offs, out):
                 else:
                     nc.scalar.activation(y_sb[piece][:, k, :], y_ps[:], RELU)
 
-        z_sb = [held.tile([P, CHUNK], BF16, name=f"z_sb{chunk}") for chunk in range(CHUNKS)]
-        for chunk in range(CHUNKS):
+        logits_ps = {}
+
+        def add_residual(piece, b, start, stop):
+            nc.tensor.matmul(logits_ps[piece, b][:], unemb_sb[:, b * P : (b + 1) * P], picked_columns(piece), start=start, stop=stop)
+
+        def make_z(chunk):
             piece, first = divmod(chunk * CHUNK, PIECE)
             z_ps = banks.tile([P, PIECE], F32, tag="bank")
             for k in range(HIDDEN_BLOCKS):
                 nc.tensor.matmul(z_ps[:, :CHUNK], mlp1_sb[:, k, :], y_sb[piece][:, k, first : first + CHUNK], start=(k == 0), stop=(k == HIDDEN_BLOCKS - 1))
+            z = held.tile([P, CHUNK], BF16, name=f"z_sb{chunk}")
             if chunk % 2 == 0:
-                nc.vector.tensor_copy(z_sb[chunk][:], z_ps[:, :CHUNK])
+                nc.vector.tensor_copy(z[:], z_ps[:, :CHUNK])
             else:
-                nc.scalar.activation(z_sb[chunk][:], z_ps[:, :CHUNK], COPY)
+                nc.scalar.activation(z[:], z_ps[:, :CHUNK], COPY)
+            return z
 
-        logits_ps = {}
-        for piece in range(PIECES):
+        def add_block(piece, part, z, start, stop):
             for b in range(LOGIT_BLOCKS):
-                logits_ps[piece, b] = banks.tile([P, PIECE], F32, name=f"logits_ps{piece}{b}", tag="bank")
-            for part in range(CHUNKS_IN_PIECE):
-                for b in range(LOGIT_BLOCKS):
-                    nc.tensor.matmul(
-                        logits_ps[piece, b][:, part * CHUNK : (part + 1) * CHUNK],
-                        unemb_sb[:, b * P : (b + 1) * P],
-                        z_sb[piece * CHUNKS_IN_PIECE + part][:],
-                        start=(part == 0),
-                        stop=False,
-                    )
+                nc.tensor.matmul(logits_ps[piece, b][:, part * CHUNK : (part + 1) * CHUNK], unemb_sb[:, b * P : (b + 1) * P], z[:], start=start, stop=stop)
 
-        for piece in range(PIECES):
-            for b in range(LOGIT_BLOCKS):
-                nc.tensor.matmul(logits_ps[piece, b][:], unemb_sb[:, b * P : (b + 1) * P], picked_columns(piece), start=False, stop=True)
-                out_sb = staged.tile([P, PIECE], F32, name="out_sb")
-                if b % 2 == 0:
-                    nc.vector.tensor_scalar_add(out_sb[:], logits_ps[piece, b][:], bias_sb[:, b : b + 1])
-                else:
-                    nc.scalar.activation(out_sb[:], logits_ps[piece, b][:], IDENTITY, bias=bias_sb[:, b : b + 1])
-                nc.sync.dma_start(out[b * P : (b + 1) * P, piece * PIECE : (piece + 1) * PIECE], out_sb[:])
+        def store(piece, b):
+            out_sb = staged.tile([P, PIECE], F32, name="out_sb")
+            if b % 2 == 0:
+                nc.vector.tensor_scalar_add(out_sb[:], logits_ps[piece, b][:], bias_sb[:, b : b + 1])
+            else:
+                nc.scalar.activation(out_sb[:], logits_ps[piece, b][:], IDENTITY, bias=bias_sb[:, b : b + 1])
+            nc.sync.dma_start(out[b * P : (b + 1) * P, piece * PIECE : (piece + 1) * PIECE], out_sb[:])
+
+        for b in range(LOGIT_BLOCKS):
+            logits_ps[0, b] = banks.tile([P, PIECE], F32, name=f"logits_ps0{b}", tag="bank")
+            add_residual(0, b, start=True, stop=False)
+
+        z_sb = [make_z(chunk) for chunk in range(CHUNKS)]
+        for part in range(CHUNKS_IN_PIECE):
+            add_block(0, part, z_sb[part], start=False, stop=(part == CHUNKS_IN_PIECE - 1))
+        for b in range(LOGIT_BLOCKS):
+            store(0, b)
+
+        for b in range(LOGIT_BLOCKS):
+            logits_ps[1, b] = banks.tile([P, PIECE], F32, name=f"logits_ps1{b}", tag="bank")
+        for part in range(CHUNKS_IN_PIECE):
+            add_block(1, part, z_sb[CHUNKS_IN_PIECE + part], start=(part == 0), stop=False)
+        for b in range(LOGIT_BLOCKS):
+            add_residual(1, b, start=False, stop=True)
+            store(1, b)

@@ -4,6 +4,7 @@ BF16, F32, U16 = mybir.dt.bfloat16, mybir.dt.float32, mybir.dt.uint16
 RELU = mybir.ActivationFunctionType.Relu
 IDENTITY = mybir.ActivationFunctionType.Identity
 COPY = mybir.ActivationFunctionType.Copy
+ADD = mybir.AluOpType.add
 
 P = 128
 WORDS = 4096
@@ -14,7 +15,6 @@ PIECE = 512
 HIDDEN_BLOCKS = HIDDEN // P
 LOGIT_BLOCKS = LOGITS // P
 PIECES = TOKENS // PIECE
-PIECE_OFFSET_COLUMNS = PIECE // 16
 CHUNK = 256
 CHUNKS = TOKENS // CHUNK
 CHUNKS_IN_PIECE = PIECE // CHUNK
@@ -50,15 +50,15 @@ def tile_transformermodel_kernel(tc, table, mlp0, mlp1, unemb, bias, offs, out):
         with nc.allow_non_contiguous_dma(reason="256 single float32, one to a partition"):
             nc.sync.dma_start(bias_sb[:], bias.rearrange("(b p) o -> p (b o)", p=P))
 
-        def picked_columns(piece):
-            return table_sb[:].indirect(offsets[:, piece * PIECE_OFFSET_COLUMNS : (piece + 1) * PIECE_OFFSET_COLUMNS])
+        def picked_columns(first_token, tokens):
+            return table_sb[:].indirect(offsets[:, first_token // 16 : (first_token + tokens) // 16])
 
 
         y_sb = [held.tile([P, HIDDEN_BLOCKS, PIECE], BF16, name=f"y_sb{piece}") for piece in range(PIECES)]
         for piece in range(PIECES):
             for k in range(HIDDEN_BLOCKS):
                 y_ps = banks.tile([P, PIECE], F32, tag="bank")
-                nc.tensor.matmul(y_ps[:], mlp0_sb[:, k * P : (k + 1) * P], picked_columns(piece))
+                nc.tensor.matmul(y_ps[:], mlp0_sb[:, k * P : (k + 1) * P], picked_columns(piece * PIECE, PIECE))
                 if k % 2 == 0:
                     nc.vector.tensor_scalar_max(y_sb[piece][:, k, :], y_ps[:], 0.0)
                 else:
@@ -67,7 +67,7 @@ def tile_transformermodel_kernel(tc, table, mlp0, mlp1, unemb, bias, offs, out):
         logits_ps = {}
 
         def add_residual(piece, b, start, stop):
-            nc.tensor.matmul(logits_ps[piece, b][:], unemb_sb[:, b * P : (b + 1) * P], picked_columns(piece), start=start, stop=stop)
+            nc.tensor.matmul(logits_ps[piece, b][:], unemb_sb[:, b * P : (b + 1) * P], picked_columns(piece * PIECE, PIECE), start=start, stop=stop)
 
         def make_z(chunk):
             piece, first = divmod(chunk * CHUNK, PIECE)
@@ -81,32 +81,46 @@ def tile_transformermodel_kernel(tc, table, mlp0, mlp1, unemb, bias, offs, out):
                 nc.scalar.activation(z[:], z_ps[:, :CHUNK], COPY)
             return z
 
-        def add_block(piece, part, z, start, stop):
-            for b in range(LOGIT_BLOCKS):
-                nc.tensor.matmul(logits_ps[piece, b][:, part * CHUNK : (part + 1) * CHUNK], unemb_sb[:, b * P : (b + 1) * P], z[:], start=start, stop=stop)
+        def add_block(piece, b, part, z, start, stop):
+            nc.tensor.matmul(logits_ps[piece, b][:, part * CHUNK : (part + 1) * CHUNK], unemb_sb[:, b * P : (b + 1) * P], z[:], start=start, stop=stop)
 
-        def store(piece, b):
+        def store(first_token, b, tokens_sb):
+            nc.sync.dma_start(out[b * P : (b + 1) * P, first_token : first_token + tokens_sb.shape[1]], tokens_sb[:])
+
+        def leave_psum(piece, b, through_vector):
             out_sb = staged.tile([P, PIECE], F32, name="out_sb")
-            if b % 2 == 0:
+            if through_vector:
                 nc.vector.tensor_scalar_add(out_sb[:], logits_ps[piece, b][:], bias_sb[:, b : b + 1])
             else:
                 nc.scalar.activation(out_sb[:], logits_ps[piece, b][:], IDENTITY, bias=bias_sb[:, b : b + 1])
-            nc.sync.dma_start(out[b * P : (b + 1) * P, piece * PIECE : (piece + 1) * PIECE], out_sb[:])
+            return out_sb
 
         for b in range(LOGIT_BLOCKS):
             logits_ps[0, b] = banks.tile([P, PIECE], F32, name=f"logits_ps0{b}", tag="bank")
             add_residual(0, b, start=True, stop=False)
 
         z_sb = [make_z(chunk) for chunk in range(CHUNKS)]
-        for part in range(CHUNKS_IN_PIECE):
-            add_block(0, part, z_sb[part], start=False, stop=(part == CHUNKS_IN_PIECE - 1))
         for b in range(LOGIT_BLOCKS):
-            store(0, b)
+            for part in range(CHUNKS_IN_PIECE):
+                add_block(0, b, part, z_sb[part], start=False, stop=(part == CHUNKS_IN_PIECE - 1))
+        for b in range(LOGIT_BLOCKS):
+            store(0, b, leave_psum(0, b, through_vector=(b == 0)))
 
         for b in range(LOGIT_BLOCKS):
             logits_ps[1, b] = banks.tile([P, PIECE], F32, name=f"logits_ps1{b}", tag="bank")
         for part in range(CHUNKS_IN_PIECE):
-            add_block(1, part, z_sb[CHUNKS_IN_PIECE + part], start=(part == 0), stop=False)
-        for b in range(LOGIT_BLOCKS):
-            add_residual(1, b, start=False, stop=True)
-            store(1, b)
+            for b in range(LOGIT_BLOCKS):
+                add_block(1, b, part, z_sb[CHUNKS_IN_PIECE + part], start=(part == 0), stop=(b == 1 and part == CHUNKS_IN_PIECE - 1))
+        block_share = leave_psum(1, 1, through_vector=True)
+
+        add_residual(1, 0, start=False, stop=True)
+        store(PIECE, 0, leave_psum(1, 0, through_vector=False))
+
+        first_token = PIECE
+        for width in (PIECE // 2, PIECE // 4, PIECE // 4):
+            residual_ps = banks.tile([P, PIECE], F32, tag="bank")
+            nc.tensor.matmul(residual_ps[:, :width], unemb_sb[:, P:], picked_columns(first_token, width))
+            part_sb = staged.tile([P, width], F32, name=f"part_sb{first_token}")
+            nc.vector.tensor_tensor(part_sb[:], residual_ps[:, :width], block_share[:, first_token - PIECE : first_token - PIECE + width], ADD)
+            store(first_token, 1, part_sb)
+            first_token += width

@@ -116,11 +116,9 @@ def tile_transformermodel_kernel(tc, table, mlp0, mlp1, unemb, bias, offs, out):
         add_residual(1, 0, start=False, stop=True)
         store(PIECE, 0, leave_psum(1, 0, through_vector=False))
 
-        first_token = PIECE
-        for width in (PIECE // 2, PIECE // 4, PIECE // 4):
+        for part in range(CHUNKS_IN_PIECE):
             residual_ps = banks.tile([P, PIECE], F32, tag="bank")
-            nc.tensor.matmul(residual_ps[:, :width], unemb_sb[:, P:], picked_columns(first_token, width))
-            part_sb = staged.tile([P, width], F32, name=f"part_sb{first_token}")
-            nc.vector.tensor_tensor(part_sb[:], residual_ps[:, :width], block_share[:, first_token - PIECE : first_token - PIECE + width], ADD)
-            store(first_token, 1, part_sb)
-            first_token += width
+            nc.tensor.matmul(residual_ps[:, :CHUNK], unemb_sb[:, P:], picked_columns(PIECE + part * CHUNK, CHUNK))
+            part_sb = staged.tile([P, CHUNK], F32, name=f"part_sb{part}")
+            nc.vector.tensor_tensor(part_sb[:], residual_ps[:, :CHUNK], block_share[:, part * CHUNK : (part + 1) * CHUNK], ADD)
+            store(PIECE + part * CHUNK, 1, part_sb)

import concourse.mybir as mybir

BF16, F32, U16 = mybir.dt.bfloat16, mybir.dt.float32, mybir.dt.uint16
RELU = mybir.ActivationFunctionType.Relu
IDENTITY = mybir.ActivationFunctionType.Identity
COPY = mybir.ActivationFunctionType.Copy
ADD = mybir.AluOpType.add

P = 128
WORDS = 4096
HIDDEN = 512
LOGITS = 256
TOKENS = 1024
PIECE = 512
HIDDEN_BLOCKS = HIDDEN // P
LOGIT_BLOCKS = LOGITS // P
PIECES = TOKENS // PIECE
CHUNK = 256
CHUNKS = TOKENS // CHUNK
CHUNKS_IN_PIECE = PIECE // CHUNK
PSUM_BANKS = 8

FLOPS = 2 * TOKENS * (P * HIDDEN + HIDDEN * P + P * LOGITS)
BYTES = 2 * (P * TOKENS + P * HIDDEN + HIDDEN * P + P * LOGITS) + 4 * LOGITS + 2 * P * (TOKENS // 16) + 4 * LOGITS * TOKENS


def tile_transformermodel_kernel(tc, table, mlp0, mlp1, unemb, bias, offs, out):
    nc = tc.nc
    with (
        tc.tile_pool(name="held", bufs=1) as held,
        tc.tile_pool(name="staged", bufs=PIECES * LOGIT_BLOCKS) as staged,
        tc.psum_pool(name="banks", bufs=PSUM_BANKS) as banks,
    ):
        offsets = held.tile([P, TOKENS // 16], U16, name="offsets")
        nc.sync.dma_start(offsets[:], offs)
        mlp0_sb = held.tile([P, HIDDEN], BF16, name="mlp0_sb")
        nc.sync.dma_start(mlp0_sb[:], mlp0)
        table_sb = held.tile([P, WORDS], BF16, name="table_sb")
        nc.scalar.dma_start(table_sb[:, WORDS // 2 :], table[:, WORDS // 2 :])
        nc.sync.dma_start(table_sb[:, : WORDS // 2], table[:, : WORDS // 2])
        table_has_landed = table_sb[:, :: WORDS // 2]
        mlp1_sb = held.tile([P, HIDDEN_BLOCKS, P], BF16, name="mlp1_sb")
        nc.vector.tensor_copy(mlp1_sb[:, 0, :2], table_has_landed)
        nc.sync.dma_start(mlp1_sb[:], mlp1.rearrange("(k p) d -> p k d", p=P))
        unemb_sb = held.tile([P, LOGITS], BF16, name="unemb_sb")
        nc.vector.tensor_copy(unemb_sb[:, :2], table_has_landed)
        nc.sync.dma_start(unemb_sb[:], unemb)
        bias_sb = held.tile([P, LOGIT_BLOCKS], F32, name="bias_sb")
        nc.vector.tensor_copy(bias_sb[:], table_has_landed)
        with nc.allow_non_contiguous_dma(reason="256 single float32, one to a partition"):
            nc.sync.dma_start(bias_sb[:], bias.rearrange("(b p) o -> p (b o)", p=P))

        def picked_columns(first_token, tokens):
            return table_sb[:].indirect(offsets[:, first_token // 16 : (first_token + tokens) // 16])


        y_sb = [held.tile([P, HIDDEN_BLOCKS, PIECE], BF16, name=f"y_sb{piece}") for piece in range(PIECES)]
        for piece in range(PIECES):
            for k in range(HIDDEN_BLOCKS):
                y_ps = banks.tile([P, PIECE], F32, tag="bank")
                nc.tensor.matmul(y_ps[:], mlp0_sb[:, k * P : (k + 1) * P], picked_columns(piece * PIECE, PIECE))
                if k % 2 == 0:
                    nc.vector.tensor_scalar_max(y_sb[piece][:, k, :], y_ps[:], 0.0)
                else:
                    nc.scalar.activation(y_sb[piece][:, k, :], y_ps[:], RELU)

        logits_ps = {}

        def add_residual(piece, b, start, stop):
            nc.tensor.matmul(logits_ps[piece, b][:], unemb_sb[:, b * P : (b + 1) * P], picked_columns(piece * PIECE, PIECE), start=start, stop=stop)

        def make_z(chunk):
            piece, first = divmod(chunk * CHUNK, PIECE)
            z_ps = banks.tile([P, PIECE], F32, tag="bank")
            for k in range(HIDDEN_BLOCKS):
                nc.tensor.matmul(z_ps[:, :CHUNK], mlp1_sb[:, k, :], y_sb[piece][:, k, first : first + CHUNK], start=(k == 0), stop=(k == HIDDEN_BLOCKS - 1))
            z = held.tile([P, CHUNK], BF16, name=f"z_sb{chunk}")
            if chunk % 2 == 0:
                nc.vector.tensor_copy(z[:], z_ps[:, :CHUNK])
            else:
                nc.scalar.activation(z[:], z_ps[:, :CHUNK], COPY)
            return z

        def add_block(piece, b, part, z, start, stop):
            nc.tensor.matmul(logits_ps[piece, b][:, part * CHUNK : (part + 1) * CHUNK], unemb_sb[:, b * P : (b + 1) * P], z[:], start=start, stop=stop)

        def store(first_token, b, tokens_sb):
            nc.sync.dma_start(out[b * P : (b + 1) * P, first_token : first_token + tokens_sb.shape[1]], tokens_sb[:])

        def leave_psum(piece, b, through_vector):
            out_sb = staged.tile([P, PIECE], F32, name="out_sb")
            if through_vector:
                nc.vector.tensor_scalar_add(out_sb[:], logits_ps[piece, b][:], bias_sb[:, b : b + 1])
            else:
                nc.scalar.activation(out_sb[:], logits_ps[piece, b][:], IDENTITY, bias=bias_sb[:, b : b + 1])
            return out_sb

        for b in range(LOGIT_BLOCKS):
            logits_ps[0, b] = banks.tile([P, PIECE], F32, name=f"logits_ps0{b}", tag="bank")
            add_residual(0, b, start=True, stop=False)

        z_sb = [make_z(chunk) for chunk in range(CHUNKS)]
        for b in range(LOGIT_BLOCKS):
            for part in range(CHUNKS_IN_PIECE):
                add_block(0, b, part, z_sb[part], start=False, stop=(part == CHUNKS_IN_PIECE - 1))
        for b in range(LOGIT_BLOCKS):
            store(0, b, leave_psum(0, b, through_vector=(b == 0)))

        for b in range(LOGIT_BLOCKS):
            logits_ps[1, b] = banks.tile([P, PIECE], F32, name=f"logits_ps1{b}", tag="bank")
        for part in range(CHUNKS_IN_PIECE):
            for b in range(LOGIT_BLOCKS):
                add_block(1, b, part, z_sb[CHUNKS_IN_PIECE + part], start=(part == 0), stop=(b == 1 and part == CHUNKS_IN_PIECE - 1))
        block_share = leave_psum(1, 1, through_vector=True)

        add_residual(1, 0, start=False, stop=True)
        store(PIECE, 0, leave_psum(1, 0, through_vector=False))

        for part in range(CHUNKS_IN_PIECE):
            residual_ps = banks.tile([P, PIECE], F32, tag="bank")
            nc.tensor.matmul(residual_ps[:, :CHUNK], unemb_sb[:, P:], picked_columns(PIECE + part * CHUNK, CHUNK))
            part_sb = staged.tile([P, CHUNK], F32, name=f"part_sb{part}")
            nc.vector.tensor_tensor(part_sb[:], residual_ps[:, :CHUNK], block_share[:, part * CHUNK : (part + 1) * CHUNK], ADD)
            store(PIECE + part * CHUNK, 1, part_sb)
